import numpy as np
import ml_dtypes


def mxq(x, axis, fmt="e4m3"):
    dtype, down = {"e4m3": (ml_dtypes.float8_e4m3fn, 7), "e5m2": (ml_dtypes.float8_e5m2, 14)}[fmt]
    v = np.moveaxis(np.asarray(x, np.float32).astype(ml_dtypes.bfloat16).astype(np.float64), axis, -1)
    blocks = v.reshape(v.shape[:-1] + (-1, 32))
    amax = np.abs(blocks).max(-1, keepdims=True)
    byte = np.maximum(np.where(amax > 0, np.frexp(amax)[1] - 1 + 127, 0) - down, 1)
    scale = np.exp2(byte - 127.0)
    codes = (blocks / scale).astype(np.float32).astype(dtype).astype(np.float64)
    return np.moveaxis((codes * scale).reshape(v.shape), -1, axis)


WIDE = False


def mx_kscale(k):
    if not WIDE:
        return np.ones(k)
    levels = np.array([10, -10, 5, -5, 0])
    if k % 512:
        return np.exp2(np.random.permutation(np.resize(levels, k // 32))).repeat(32)
    a = np.empty((k // 512, 16))
    for p in range(k // 512):
        a[p, :8] = np.random.permutation(np.resize(levels, 8))
        for g in range(8):
            far = levels[np.abs(levels - a[p, g]) >= 10]
            a[p, g + 8] = far[np.random.randint(len(far))]
    return np.exp2(a.ravel()).repeat(32)


BF16 = ml_dtypes.bfloat16


def bf(x):
    return np.asarray(x, np.float32).astype(BF16)


def f64(x):
    return np.asarray(x).astype(np.float64)


B, F, O = 8192, 1024, 128


def setup_inputs():
    s = mx_kscale(F)
    return {"x": bf(np.random.standard_normal((B, 2, F)) * s),
            "filters_real": bf(np.random.standard_normal((O, F)) * 0.5 / np.sqrt(F) / s),
            "filters_imag": bf(np.random.standard_normal((O, F)) * 0.5 / np.sqrt(F) / s)}


def reference(x, filters_real, filters_imag):
    x = f64(x)
    x_real = x[:, 0]
    x_imag = x[:, 1]
    w_r = f64(filters_real) + f64(filters_imag)
    w_i = f64(filters_real) - f64(filters_imag)
    energies = (mxq(x_real, 1, "e4m3") @ mxq(w_r, 1, "e4m3").T) + (mxq(x_imag, 1, "e4m3") @ mxq(w_i, 1, "e4m3").T)
    return energies

@@ -1,0 +1,164 @@
+from contextlib import ExitStack
+
+import concourse.mybir as mybir
+from concourse.masks import make_identity
+
+FLOPS = 2 * 8192 * 2048 * 128
+
+F32 = mybir.dt.float32
+BF16 = mybir.dt.bfloat16
+U32 = mybir.dt.uint32
+U8 = mybir.dt.uint8
+FP8X4 = mybir.dt.float8_e4m3fn_x4
+ADD = mybir.AluOpType.add
+SUB = mybir.AluOpType.subtract
+
+P = 128
+K = 2048
+PASSES = 4
+GROUP_TILES = [1, 1, 2] + [4] * 14 + [2, 1, 1]
+X_BUFS = 8
+PIN = True
+RUN = 2
+
+
+def tile_fftmlp_t_kernel(tc, x, filters_real, filters_imag, out):
+    nc = tc.nc
+    n_groups = len(GROUP_TILES)
+    bases = [P * sum(GROUP_TILES[:gi]) for gi in range(n_groups)]
+    row_tiles = [(gi, t) for gi in range(n_groups) for t in range(GROUP_TILES[gi])]
+    n_rt = len(row_tiles)
+    assert n_rt * P == x.shape[0]
+
+    with ExitStack() as ctx:
+        consts = ctx.enter_context(tc.tile_pool(name="consts", bufs=1))
+        xpool = ctx.enter_context(tc.tile_pool(name="xpool", bufs=X_BUFS))
+        gpool = ctx.enter_context(tc.tile_pool(name="gpool", bufs=4))
+        qpool = ctx.enter_context(tc.tile_pool(name="qpool", bufs=6))
+        opool = ctx.enter_context(tc.tile_pool(name="opool", bufs=len(GROUP_TILES)))
+        psum_t = ctx.enter_context(tc.psum_pool(name="psum_t", bufs=6))
+        psum_o = ctx.enter_context(tc.psum_pool(name="psum_o", bufs=2))
+        if PIN:
+            ctx.enter_context(tc.manual_schedule())
+
+        x_tiles = {}
+        banks = {}
+        grouped = {}
+        codes = {}
+        scales = {}
+        o_banks = {}
+
+        def load(gi):
+            n_t = GROUP_TILES[gi]
+            x_sb = xpool.tile([P, n_t * K], BF16, tag="x", name="x_sb")
+            rows = x[bases[gi] : bases[gi] + P * n_t]
+            nc.sync.dma_start(out=x_sb[:], in_=rows.rearrange("(p t) c f -> p (t c f)", t=n_t))
+            x_tiles[gi] = x_sb
+
+        def transposes(r):
+            gi, t = row_tiles[r]
+            words = x_tiles[gi][:].bitcast(F32)
+            for h in range(2):
+                bank = psum_t.tile([P, 4, P], F32, tag="xt", name="bank")
+                for j in range(4):
+                    w0 = t * (K // 2) + (2 * h + j // 2) * 2 * P
+                    nc.tensor.transpose(bank[:, j, :], words[:, w0 + j % 2 : w0 + 2 * P : 2], ident_f32[:])
+                banks[(r, h)] = bank
+
+        def copy_out(r, h, on_vector):
+            if h == 0:
+                grouped[r] = gpool.tile([P, 4 * PASSES * P], BF16, tag="grouped", name="grouped", align_bytes=64)
+            dst = grouped[r][:].bitcast(F32).rearrange("p (g r u) -> p g r u", g=PASSES, u=2)
+            src = banks[(r, h)][:].rearrange("p (g u) r -> p g r u", u=2)
+            if on_vector:
+                nc.vector.tensor_copy(out=dst[:, 2 * h : 2 * h + 2], in_=src)
+            else:
+                nc.scalar.copy(out=dst[:, 2 * h : 2 * h + 2], in_=src)
+
+        def quantise(r):
+            codes[r] = qpool.tile([P, PASSES * P], U32, tag="codes", name="codes", align_bytes=64)
+            scales[r] = qpool.tile([P, PASSES * P], U8, tag="scales", name="scales", align_bytes=64)
+            nc.vector.quantize_mx(out=codes[r][:].bitcast(FP8X4), scales=scales[r][:], in_=grouped[r][:])
+
+        def multiply(r):
+            gi, t = row_tiles[r]
+            if t == 0:
+                o_banks[gi] = psum_o.tile([P, 4 * P], F32, tag="o", name="o_bank")
+            for g in range(PASSES):
+                cols = slice(g * P, (g + 1) * P)
+                nc.tensor.matmul_mx(
+                    out=o_banks[gi][:, t * P : (t + 1) * P],
+                    lhsT=codes[r][:, cols].bitcast(FP8X4),
+                    lhsT_scale=scales[r][:, cols],
+                    rhs=w_codes[:, cols].bitcast(FP8X4),
+                    rhs_scale=w_scales[:, cols],
+                    start=(g == 0),
+                    stop=(g == PASSES - 1),
+                )
+            if t == GROUP_TILES[gi] - 1:
+                n_t = GROUP_TILES[gi]
+                o_sb = opool.tile([P, 4 * P], F32, tag="o_sb", name="o_sb")
+                nc.scalar.copy(out=o_sb[:, : n_t * P], in_=o_banks[gi][:, : n_t * P])
+                rows = out[bases[gi] : bases[gi] + P * n_t, :]
+                nc.sync.dma_start(out=rows.rearrange("(p t) o -> p (t o)", t=n_t), in_=o_sb[:, : n_t * P])
+
+        fr = consts.tile([P, 1024], BF16, name="fr")
+        fi = consts.tile([P, 1024], BF16, name="fi")
+        nc.sync.dma_start(out=fr[:], in_=filters_real)
+        nc.sync.dma_start(out=fi[:], in_=filters_imag)
+        for gi in range(X_BUFS):
+            load(gi)
+        loaded = [X_BUFS]
+
+        ident_f32 = consts.tile([P, P], F32, name="ident_f32")
+        make_identity(nc, ident_f32[:])
+        ident_bf = consts.tile([P, P], BF16, name="ident_bf")
+        make_identity(nc, ident_bf[:])
+
+        w_perm = consts.tile([P, 2, 8, P], BF16, name="w_perm")
+        for c, op in ((0, ADD), (1, SUB)):
+            nc.vector.tensor_tensor(
+                out=w_perm[:, c].rearrange("o (g t) p -> o g t p", t=4),
+                in0=fr[:].rearrange("o (g p t) -> o g t p", g=2, t=4),
+                in1=fi[:].rearrange("o (g p t) -> o g t p", g=2, t=4),
+                op=op,
+            )
+        w_grouped = consts.tile([P, 4 * PASSES * P], BF16, name="w_grouped", align_bytes=64)
+        w_codes = consts.tile([P, PASSES * P], U32, name="w_codes", align_bytes=64)
+        w_scales = consts.tile([P, PASSES * P], U8, name="w_scales", align_bytes=64)
+
+        def weights():
+            w_dst = w_grouped[:].rearrange("p (g o t) -> p g o t", g=PASSES, t=4)
+            for c in range(2):
+                w_bank = psum_t.tile([P, 8, P], BF16, tag="xt", name="w_bank")
+                for j in range(8):
+                    nc.tensor.transpose(w_bank[:, j, :], w_perm[:, c, j, :], ident_bf[:])
+                w_src = w_bank[:].rearrange("p (g t) o -> p g o t", t=4)
+                if c == 0:
+                    nc.scalar.copy(out=w_dst[:, 0:2], in_=w_src)
+                else:
+                    nc.vector.tensor_copy(out=w_dst[:, 2:4], in_=w_src)
+            nc.vector.quantize_mx(out=w_codes[:].bitcast(FP8X4), scales=w_scales[:], in_=w_grouped[:])
+
+        n_steps = n_rt // RUN
+        for b in range(n_steps + 1):
+            run = list(range(b * RUN, (b + 1) * RUN)) if b < n_steps else []
+            for r in run:
+                transposes(r)
+                gi, t = row_tiles[r]
+                if t == GROUP_TILES[gi] - 1 and loaded[0] < n_groups:
+                    load(loaded[0])
+                    loaded[0] += 1
+            if b > 0 and (b * RUN - 1) not in codes:
+                quantise(b * RUN - 1)
+            for r in run:
+                copy_out(r, 0, False)
+                vec = (r % 2 == 0) or (r == n_rt - 1)
+                copy_out(r, 1, vec)
+                if vec:
+                    quantise(r)
+            if b == 0:
+                weights()
+            if b > 0:
+                for r in range((b - 1) * RUN, b * RUN):
+                    multiply(r)

@@ -15,11 +15,12 @@ SUB = mybir.AluOpType.subtract
 
 P = 128
 K = 2048
+WORDS = K // 2
 PASSES = 4
 GROUP_TILES = [1, 1, 2] + [4] * 14 + [2, 1, 1]
 X_BUFS = 8
-PIN = True
 RUN = 2
+W = -1
 
 
 def tile_fftmlp_t_kernel(tc, x, filters_real, filters_imag, out):
@@ -33,15 +34,16 @@ def tile_fftmlp_t_kernel(tc, x, filters_real, filters_imag, out):
     with ExitStack() as ctx:
         consts = ctx.enter_context(tc.tile_pool(name="consts", bufs=1))
         xpool = ctx.enter_context(tc.tile_pool(name="xpool", bufs=X_BUFS))
+        ppool = ctx.enter_context(tc.tile_pool(name="ppool", bufs=5))
         gpool = ctx.enter_context(tc.tile_pool(name="gpool", bufs=4))
         qpool = ctx.enter_context(tc.tile_pool(name="qpool", bufs=6))
-        opool = ctx.enter_context(tc.tile_pool(name="opool", bufs=len(GROUP_TILES)))
+        opool = ctx.enter_context(tc.tile_pool(name="opool", bufs=12))
         psum_t = ctx.enter_context(tc.psum_pool(name="psum_t", bufs=6))
         psum_o = ctx.enter_context(tc.psum_pool(name="psum_o", bufs=2))
-        if PIN:
-            ctx.enter_context(tc.manual_schedule())
+        ctx.enter_context(tc.manual_schedule())
 
         x_tiles = {}
+        perms = {}
         banks = {}
         grouped = {}
         codes = {}
@@ -55,14 +57,27 @@ def tile_fftmlp_t_kernel(tc, x, filters_real, filters_imag, out):
             nc.sync.dma_start(out=x_sb[:], in_=rows.rearrange("(p t) c f -> p (t c f)", t=n_t))
             x_tiles[gi] = x_sb
 
-        def transposes(r):
+        loaded = [0]
+
+        def permute(r):
             gi, t = row_tiles[r]
-            words = x_tiles[gi][:].bitcast(F32)
+            perms[r] = ppool.tile([P, K], BF16, tag="perm", name="perm")
+            nc.vector.tensor_copy(
+                out=perms[r][:].rearrange("p (u b e) -> p u b e", u=2, e=16),
+                in_=x_tiles[gi][:, t * K : (t + 1) * K].rearrange("p (b u e) -> p u b e", u=2, e=16),
+            )
+            if t == GROUP_TILES[gi] - 1 and loaded[0] < n_groups:
+                load(loaded[0])
+                loaded[0] += 1
+
+        def transposes(r):
+            words = perms[r][:].bitcast(F32)
             for h in range(2):
                 bank = psum_t.tile([P, 4, P], F32, tag="xt", name="bank")
                 for j in range(4):
-                    w0 = t * (K // 2) + (2 * h + j // 2) * 2 * P
-                    nc.tensor.transpose(bank[:, j, :], words[:, w0 + j % 2 : w0 + 2 * P : 2], ident_f32[:])
+                    g, u = 2 * h + j // 2, j % 2
+                    w0 = u * (WORDS // 2) + g * P
+                    nc.tensor.transpose(bank[:, j, :], words[:, w0 : w0 + P], ident_f32[:])
                 banks[(r, h)] = bank
 
         def copy_out(r, h, on_vector):
@@ -76,8 +91,10 @@ def tile_fftmlp_t_kernel(tc, x, filters_real, filters_imag, out):
                 nc.scalar.copy(out=dst[:, 2 * h : 2 * h + 2], in_=src)
 
         def quantise(r):
-            codes[r] = qpool.tile([P, PASSES * P], U32, tag="codes", name="codes", align_bytes=64)
-            scales[r] = qpool.tile([P, PASSES * P], U8, tag="scales", name="scales", align_bytes=64)
+            pool = consts if r == W else qpool
+            tag = "w_" if r == W else ""
+            codes[r] = pool.tile([P, PASSES * P], U32, tag=tag + "codes", name="codes", align_bytes=64)
+            scales[r] = pool.tile([P, PASSES * P], U8, tag=tag + "scales", name="scales", align_bytes=64)
             nc.vector.quantize_mx(out=codes[r][:].bitcast(FP8X4), scales=scales[r][:], in_=grouped[r][:])
 
         def multiply(r):
@@ -90,75 +107,63 @@ def tile_fftmlp_t_kernel(tc, x, filters_real, filters_imag, out):
                     out=o_banks[gi][:, t * P : (t + 1) * P],
                     lhsT=codes[r][:, cols].bitcast(FP8X4),
                     lhsT_scale=scales[r][:, cols],
-                    rhs=w_codes[:, cols].bitcast(FP8X4),
-                    rhs_scale=w_scales[:, cols],
+                    rhs=codes[W][:, cols].bitcast(FP8X4),
+                    rhs_scale=scales[W][:, cols],
                     start=(g == 0),
                     stop=(g == PASSES - 1),
                 )
             if t == GROUP_TILES[gi] - 1:
                 n_t = GROUP_TILES[gi]
                 o_sb = opool.tile([P, 4 * P], F32, tag="o_sb", name="o_sb")
-                nc.scalar.copy(out=o_sb[:, : n_t * P], in_=o_banks[gi][:, : n_t * P])
+                if gi % 2 == 0:
+                    nc.vector.tensor_copy(out=o_sb[:, : n_t * P], in_=o_banks[gi][:, : n_t * P])
+                else:
+                    nc.scalar.copy(out=o_sb[:, : n_t * P], in_=o_banks[gi][:, : n_t * P])
                 rows = out[bases[gi] : bases[gi] + P * n_t, :]
                 nc.sync.dma_start(out=rows.rearrange("(p t) o -> p (t o)", t=n_t), in_=o_sb[:, : n_t * P])
 
+        load(0)
         fr = consts.tile([P, 1024], BF16, name="fr")
         fi = consts.tile([P, 1024], BF16, name="fi")
         nc.sync.dma_start(out=fr[:], in_=filters_real)
         nc.sync.dma_start(out=fi[:], in_=filters_imag)
-        for gi in range(X_BUFS):
+        for gi in range(1, X_BUFS):
             load(gi)
-        loaded = [X_BUFS]
+        loaded[0] = X_BUFS
 
         ident_f32 = consts.tile([P, P], F32, name="ident_f32")
         make_identity(nc, ident_f32[:])
-        ident_bf = consts.tile([P, P], BF16, name="ident_bf")
-        make_identity(nc, ident_bf[:])
 
-        w_perm = consts.tile([P, 2, 8, P], BF16, name="w_perm")
+        permute(0)
+        perms[W] = ppool.tile([P, K], BF16, tag="perm", name="perm")
+        w_dst = perms[W][:].rearrange("o (u c b e) -> o c u b e", u=2, c=2, e=16)
         for c, op in ((0, ADD), (1, SUB)):
             nc.vector.tensor_tensor(
-                out=w_perm[:, c].rearrange("o (g t) p -> o g t p", t=4),
-                in0=fr[:].rearrange("o (g p t) -> o g t p", g=2, t=4),
-                in1=fi[:].rearrange("o (g p t) -> o g t p", g=2, t=4),
+                out=w_dst[:, c],
+                in0=fr[:].rearrange("o (b u e) -> o u b e", u=2, e=16),
+                in1=fi[:].rearrange("o (b u e) -> o u b e", u=2, e=16),
                 op=op,
             )
-        w_grouped = consts.tile([P, 4 * PASSES * P], BF16, name="w_grouped", align_bytes=64)
-        w_codes = consts.tile([P, PASSES * P], U32, name="w_codes", align_bytes=64)
-        w_scales = consts.tile([P, PASSES * P], U8, name="w_scales", align_bytes=64)
-
-        def weights():
-            w_dst = w_grouped[:].rearrange("p (g o t) -> p g o t", g=PASSES, t=4)
-            for c in range(2):
-                w_bank = psum_t.tile([P, 8, P], BF16, tag="xt", name="w_bank")
-                for j in range(8):
-                    nc.tensor.transpose(w_bank[:, j, :], w_perm[:, c, j, :], ident_bf[:])
-                w_src = w_bank[:].rearrange("p (g t) o -> p g o t", t=4)
-                if c == 0:
-                    nc.scalar.copy(out=w_dst[:, 0:2], in_=w_src)
-                else:
-                    nc.vector.tensor_copy(out=w_dst[:, 2:4], in_=w_src)
-            nc.vector.quantize_mx(out=w_codes[:].bitcast(FP8X4), scales=w_scales[:], in_=w_grouped[:])
+        permute(1)
 
         n_steps = n_rt // RUN
         for b in range(n_steps + 1):
             run = list(range(b * RUN, (b + 1) * RUN)) if b < n_steps else []
             for r in run:
                 transposes(r)
-                gi, t = row_tiles[r]
-                if t == GROUP_TILES[gi] - 1 and loaded[0] < n_groups:
-                    load(loaded[0])
-                    loaded[0] += 1
-            if b > 0 and (b * RUN - 1) not in codes:
-                quantise(b * RUN - 1)
+                if r == 0:
+                    transposes(W)
             for r in run:
+                if r + RUN < n_rt:
+                    permute(r + RUN)
                 copy_out(r, 0, False)
-                vec = (r % 2 == 0) or (r == n_rt - 1)
-                copy_out(r, 1, vec)
-                if vec:
-                    quantise(r)
-            if b == 0:
-                weights()
+                copy_out(r, 1, False)
+                if r == 0:
+                    copy_out(W, 0, True)
+                    copy_out(W, 1, True)
+                quantise(r)
+                if r == 0:
+                    quantise(W)
             if b > 0:
                 for r in range((b - 1) * RUN, b * RUN):
                     multiply(r)

@@ -35,7 +35,7 @@ def tile_fftmlp_t_kernel(tc, x, filters_real, filters_imag, out):
         consts = ctx.enter_context(tc.tile_pool(name="consts", bufs=1))
         xpool = ctx.enter_context(tc.tile_pool(name="xpool", bufs=X_BUFS))
         ppool = ctx.enter_context(tc.tile_pool(name="ppool", bufs=5))
-        gpool = ctx.enter_context(tc.tile_pool(name="gpool", bufs=4))
+        gpool = ctx.enter_context(tc.tile_pool(name="gpool", bufs=6))
         qpool = ctx.enter_context(tc.tile_pool(name="qpool", bufs=6))
         opool = ctx.enter_context(tc.tile_pool(name="opool", bufs=12))
         psum_t = ctx.enter_context(tc.psum_pool(name="psum_t", bufs=6))
@@ -147,23 +147,25 @@ def tile_fftmlp_t_kernel(tc, x, filters_real, filters_imag, out):
         permute(1)
 
         n_steps = n_rt // RUN
-        for b in range(n_steps + 1):
-            run = list(range(b * RUN, (b + 1) * RUN)) if b < n_steps else []
-            for r in run:
-                transposes(r)
-                if r == 0:
-                    transposes(W)
-            for r in run:
-                if r + RUN < n_rt:
-                    permute(r + RUN)
-                copy_out(r, 0, False)
-                copy_out(r, 1, False)
-                if r == 0:
+        runs = [list(range(b * RUN, (b + 1) * RUN)) for b in range(n_steps)]
+        for b in range(n_steps + 2):
+            if b < n_steps:
+                for r in runs[b]:
+                    transposes(r)
+                    if r == 0:
+                        transposes(W)
+            for k in range(RUN):
+                if b + 1 < n_steps:
+                    permute(runs[b + 1][k])
+                if b < n_steps:
+                    copy_out(runs[b][k], 0, False)
+                    copy_out(runs[b][k], 1, False)
+                if b == 0 and k == 0:
                     copy_out(W, 0, True)
                     copy_out(W, 1, True)
-                quantise(r)
-                if r == 0:
                     quantise(W)
-            if b > 0:
-                for r in range((b - 1) * RUN, b * RUN):
+                if 0 < b <= n_steps:
+                    quantise(runs[b - 1][k])
+            if b > 1:
+                for r in runs[b - 2]:
                     multiply(r)

@@ -17,6 +17,8 @@ P = 128
 K = 2048
 WORDS = K // 2
 PASSES = 4
+PERM_PASSES = 3
+PW = PERM_PASSES * 256
 GROUP_TILES = [1, 1, 2] + [4] * 14 + [2, 1, 1]
 X_BUFS = 8
 RUN = 2
@@ -61,24 +63,32 @@ def tile_fftmlp_t_kernel(tc, x, filters_real, filters_imag, out):
 
         def permute(r):
             gi, t = row_tiles[r]
-            perms[r] = ppool.tile([P, K], BF16, tag="perm", name="perm")
+            src = w_sum[:] if r == W else x_tiles[gi][:, t * K : (t + 1) * K]
+            perms[r] = ppool.tile([P, 2 * PW], BF16, tag="perm", name="perm")
             nc.vector.tensor_copy(
                 out=perms[r][:].rearrange("p (u b e) -> p u b e", u=2, e=16),
-                in_=x_tiles[gi][:, t * K : (t + 1) * K].rearrange("p (b u e) -> p u b e", u=2, e=16),
+                in_=src[:, : 2 * PW].rearrange("p (b u e) -> p u b e", u=2, e=16),
             )
-            if t == GROUP_TILES[gi] - 1 and loaded[0] < n_groups:
-                load(loaded[0])
-                loaded[0] += 1
 
         def transposes(r):
+            gi, t = row_tiles[r]
+            src = w_sum[:] if r == W else x_tiles[gi][:, t * K : (t + 1) * K]
+            plain = src.bitcast(F32)
             words = perms[r][:].bitcast(F32)
             for h in range(2):
                 bank = psum_t.tile([P, 4, P], F32, tag="xt", name="bank")
                 for j in range(4):
                     g, u = 2 * h + j // 2, j % 2
-                    w0 = u * (WORDS // 2) + g * P
-                    nc.tensor.transpose(bank[:, j, :], words[:, w0 : w0 + P], ident_f32[:])
+                    if g < PERM_PASSES:
+                        w0 = u * (PW // 2) + g * P
+                        in_words = words[:, w0 : w0 + P]
+                    else:
+                        in_words = plain[:, 256 * g + u : 256 * (g + 1) : 2]
+                    nc.tensor.transpose(bank[:, j, :], in_words, ident_f32[:])
                 banks[(r, h)] = bank
+            if r != W and t == GROUP_TILES[gi] - 1 and loaded[0] < n_groups:
+                load(loaded[0])
+                loaded[0] += 1
 
         def copy_out(r, h, on_vector):
             if h == 0:
@@ -135,15 +145,10 @@ def tile_fftmlp_t_kernel(tc, x, filters_real, filters_imag, out):
         make_identity(nc, ident_f32[:])
 
         permute(0)
-        perms[W] = ppool.tile([P, K], BF16, tag="perm", name="perm")
-        w_dst = perms[W][:].rearrange("o (u c b e) -> o c u b e", u=2, c=2, e=16)
-        for c, op in ((0, ADD), (1, SUB)):
-            nc.vector.tensor_tensor(
-                out=w_dst[:, c],
-                in0=fr[:].rearrange("o (b u e) -> o u b e", u=2, e=16),
-                in1=fi[:].rearrange("o (b u e) -> o u b e", u=2, e=16),
-                op=op,
-            )
+        w_sum = consts.tile([P, K], BF16, name="w_sum")
+        nc.vector.tensor_tensor(out=w_sum[:, :1024], in0=fr[:], in1=fi[:], op=ADD)
+        nc.vector.tensor_tensor(out=w_sum[:, 1024:], in0=fr[:], in1=fi[:], op=SUB)
+        permute(W)
         permute(1)
 
         n_steps = n_rt // RUN

@@ -15,36 +15,54 @@ SUB = mybir.AluOpType.subtract
 
 P = 128
 K = 2048
-WORDS = K // 2
 PASSES = 4
 PERM_PASSES = 3
 PW = PERM_PASSES * 256
-GROUP_TILES = [1, 1, 2] + [4] * 14 + [2, 1, 1]
-X_BUFS = 8
-RUN = 2
+GROUPS = [(1,), (1,), (2,), (4,)] + [(4, 4)] * 6 + [(4,), (2,), (1,), (1,)]
+STEPS = [(0,), (1,)] + [(r, r + 1) for r in range(2, 64, 2)]
+X_BUFS = 6
+PERM_AHEAD = 2
+QUANTISE_LAG = 1
+MX_LAG = 2
+OUT_SCALAR = 4
+P_BUFS = 5
+G_BUFS = 5
+Q_BUFS = 8
 W = -1
 
 
 def tile_fftmlp_t_kernel(tc, x, filters_real, filters_imag, out):
     nc = tc.nc
-    n_groups = len(GROUP_TILES)
-    bases = [P * sum(GROUP_TILES[:gi]) for gi in range(n_groups)]
-    row_tiles = [(gi, t) for gi in range(n_groups) for t in range(GROUP_TILES[gi])]
-    n_rt = len(row_tiles)
+    loads = []
+    stores = []
+    where = []
+    for group in GROUPS:
+        base, size = len(where) * P, sum(group)
+        stores.append((base, size))
+        t0 = 0
+        for n in group:
+            where += [(len(loads), k) for k in range(n)]
+            loads.append((base, size, t0, n))
+            t0 += n
+    n_rt = len(where)
     assert n_rt * P == x.shape[0]
 
     with ExitStack() as ctx:
         consts = ctx.enter_context(tc.tile_pool(name="consts", bufs=1))
         xpool = ctx.enter_context(tc.tile_pool(name="xpool", bufs=X_BUFS))
-        ppool = ctx.enter_context(tc.tile_pool(name="ppool", bufs=5))
-        gpool = ctx.enter_context(tc.tile_pool(name="gpool", bufs=6))
-        qpool = ctx.enter_context(tc.tile_pool(name="qpool", bufs=6))
-        opool = ctx.enter_context(tc.tile_pool(name="opool", bufs=12))
+        ppool = ctx.enter_context(tc.tile_pool(name="ppool", bufs=P_BUFS))
+        gpool = ctx.enter_context(tc.tile_pool(name="gpool", bufs=G_BUFS))
+        qpool = ctx.enter_context(tc.tile_pool(name="qpool", bufs=Q_BUFS))
         psum_t = ctx.enter_context(tc.psum_pool(name="psum_t", bufs=6))
         psum_o = ctx.enter_context(tc.psum_pool(name="psum_o", bufs=2))
         ctx.enter_context(tc.manual_schedule())
 
-        x_tiles = {}
+        fr = consts.tile([P, K // 2], BF16, name="fr")
+        fi = consts.tile([P, K // 2], BF16, name="fi")
+        w_sum = consts.tile([P, K], BF16, name="w_sum")
+        ident = consts.tile([P, P], F32, name="ident")
+        o_all = consts.tile([P, n_rt * P], F32, name="o_all")
+        x_tiles = []
         perms = {}
         banks = {}
         grouped = {}
@@ -52,28 +70,28 @@ def tile_fftmlp_t_kernel(tc, x, filters_real, filters_imag, out):
         scales = {}
         o_banks = {}
 
-        def load(gi):
-            n_t = GROUP_TILES[gi]
-            x_sb = xpool.tile([P, n_t * K], BF16, tag="x", name="x_sb")
-            rows = x[bases[gi] : bases[gi] + P * n_t]
-            nc.sync.dma_start(out=x_sb[:], in_=rows.rearrange("(p t) c f -> p (t c f)", t=n_t))
-            x_tiles[gi] = x_sb
+        def load():
+            base, size, t0, n = loads[len(x_tiles)]
+            x_sb = xpool.tile([P, n * K], BF16, tag="x", name="x_sb")
+            rows = x[base : base + size * P].rearrange("(p t) c f -> p t (c f)", t=size)
+            nc.sync.dma_start(out=x_sb[:].rearrange("p (t k) -> p t k", t=n), in_=rows[:, t0 : t0 + n])
+            x_tiles.append(x_sb)
 
-        loaded = [0]
+        def rows_of(r):
+            if r == W:
+                return w_sum[:]
+            i, k = where[r]
+            return x_tiles[i][:, k * K : (k + 1) * K]
 
         def permute(r):
-            gi, t = row_tiles[r]
-            src = w_sum[:] if r == W else x_tiles[gi][:, t * K : (t + 1) * K]
             perms[r] = ppool.tile([P, 2 * PW], BF16, tag="perm", name="perm")
             nc.vector.tensor_copy(
                 out=perms[r][:].rearrange("p (u b e) -> p u b e", u=2, e=16),
-                in_=src[:, : 2 * PW].rearrange("p (b u e) -> p u b e", u=2, e=16),
+                in_=rows_of(r)[:, : 2 * PW].rearrange("p (b u e) -> p u b e", u=2, e=16),
             )
 
         def transposes(r):
-            gi, t = row_tiles[r]
-            src = w_sum[:] if r == W else x_tiles[gi][:, t * K : (t + 1) * K]
-            plain = src.bitcast(F32)
+            plain = rows_of(r).bitcast(F32)
             words = perms[r][:].bitcast(F32)
             for h in range(2):
                 bank = psum_t.tile([P, 4, P], F32, tag="xt", name="bank")
@@ -84,21 +102,15 @@ def tile_fftmlp_t_kernel(tc, x, filters_real, filters_imag, out):
                         in_words = words[:, w0 : w0 + P]
                     else:
                         in_words = plain[:, 256 * g + u : 256 * (g + 1) : 2]
-                    nc.tensor.transpose(bank[:, j, :], in_words, ident_f32[:])
+                    nc.tensor.transpose(bank[:, j, :], in_words, ident[:])
                 banks[(r, h)] = bank
-            if r != W and t == GROUP_TILES[gi] - 1 and loaded[0] < n_groups:
-                load(loaded[0])
-                loaded[0] += 1
 
-        def copy_out(r, h, on_vector):
-            if h == 0:
-                grouped[r] = gpool.tile([P, 4 * PASSES * P], BF16, tag="grouped", name="grouped", align_bytes=64)
+        def copy_out(r, engine_copy):
+            grouped[r] = gpool.tile([P, 4 * PASSES * P], BF16, tag="grouped", name="grouped", align_bytes=64)
             dst = grouped[r][:].bitcast(F32).rearrange("p (g r u) -> p g r u", g=PASSES, u=2)
-            src = banks[(r, h)][:].rearrange("p (g u) r -> p g r u", u=2)
-            if on_vector:
-                nc.vector.tensor_copy(out=dst[:, 2 * h : 2 * h + 2], in_=src)
-            else:
-                nc.scalar.copy(out=dst[:, 2 * h : 2 * h + 2], in_=src)
+            for h in range(2):
+                src = banks[(r, h)][:].rearrange("p (g u) r -> p g r u", u=2)
+                engine_copy(out=dst[:, 2 * h : 2 * h + 2], in_=src)
 
         def quantise(r):
             pool = consts if r == W else qpool
@@ -107,70 +119,68 @@ def tile_fftmlp_t_kernel(tc, x, filters_real, filters_imag, out):
             scales[r] = pool.tile([P, PASSES * P], U8, tag=tag + "scales", name="scales", align_bytes=64)
             nc.vector.quantize_mx(out=codes[r][:].bitcast(FP8X4), scales=scales[r][:], in_=grouped[r][:])
 
-        def multiply(r):
-            gi, t = row_tiles[r]
-            if t == 0:
-                o_banks[gi] = psum_o.tile([P, 4 * P], F32, tag="o", name="o_bank")
-            for g in range(PASSES):
-                cols = slice(g * P, (g + 1) * P)
-                nc.tensor.matmul_mx(
-                    out=o_banks[gi][:, t * P : (t + 1) * P],
-                    lhsT=codes[r][:, cols].bitcast(FP8X4),
-                    lhsT_scale=scales[r][:, cols],
-                    rhs=codes[W][:, cols].bitcast(FP8X4),
-                    rhs_scale=scales[W][:, cols],
-                    start=(g == 0),
-                    stop=(g == PASSES - 1),
-                )
-            if t == GROUP_TILES[gi] - 1:
-                n_t = GROUP_TILES[gi]
-                o_sb = opool.tile([P, 4 * P], F32, tag="o_sb", name="o_sb")
-                if gi % 2 == 0:
-                    nc.vector.tensor_copy(out=o_sb[:, : n_t * P], in_=o_banks[gi][:, : n_t * P])
-                else:
-                    nc.scalar.copy(out=o_sb[:, : n_t * P], in_=o_banks[gi][:, : n_t * P])
-                rows = out[bases[gi] : bases[gi] + P * n_t, :]
-                nc.sync.dma_start(out=rows.rearrange("(p t) o -> p (t o)", t=n_t), in_=o_sb[:, : n_t * P])
+        def multiply(step):
+            bank = psum_o.tile([P, 4 * P], F32, tag="o", name="o_bank")
+            o_banks[step[0]] = bank
+            for k, r in enumerate(step):
+                for g in range(PASSES):
+                    cols = slice(g * P, (g + 1) * P)
+                    nc.tensor.matmul_mx(
+                        out=bank[:, k * P : (k + 1) * P],
+                        lhsT=codes[r][:, cols].bitcast(FP8X4),
+                        lhsT_scale=scales[r][:, cols],
+                        rhs=codes[W][:, cols].bitcast(FP8X4),
+                        rhs_scale=scales[W][:, cols],
+                        start=(g == 0),
+                        stop=(g == PASSES - 1),
+                    )
 
-        load(0)
-        fr = consts.tile([P, 1024], BF16, name="fr")
-        fi = consts.tile([P, 1024], BF16, name="fi")
+        def outputs(step, engine_copy):
+            r0, n = step[0], len(step)
+            engine_copy(out=o_all[:, r0 * P : (r0 + n) * P], in_=o_banks[r0][:, : n * P])
+
+        def store(base, size):
+            rows = out[base : base + size * P, :].rearrange("(p t) o -> p (t o)", t=size)
+            nc.sync.dma_start(out=rows, in_=o_all[:, base : base + size * P])
+
+        load()
         nc.sync.dma_start(out=fr[:], in_=filters_real)
         nc.sync.dma_start(out=fi[:], in_=filters_imag)
-        for gi in range(1, X_BUFS):
-            load(gi)
-        loaded[0] = X_BUFS
-
-        ident_f32 = consts.tile([P, P], F32, name="ident_f32")
-        make_identity(nc, ident_f32[:])
+        while len(x_tiles) < X_BUFS:
+            load()
+        make_identity(nc, ident[:])
 
         permute(0)
-        w_sum = consts.tile([P, K], BF16, name="w_sum")
-        nc.vector.tensor_tensor(out=w_sum[:, :1024], in0=fr[:], in1=fi[:], op=ADD)
-        nc.vector.tensor_tensor(out=w_sum[:, 1024:], in0=fr[:], in1=fi[:], op=SUB)
+        nc.vector.tensor_tensor(out=w_sum[:, : K // 2], in0=fr[:], in1=fi[:], op=ADD)
+        nc.vector.tensor_tensor(out=w_sum[:, K // 2 :], in0=fr[:], in1=fi[:], op=SUB)
         permute(W)
-        permute(1)
+        for r in range(1, PERM_AHEAD):
+            permute(r)
 
-        n_steps = n_rt // RUN
-        runs = [list(range(b * RUN, (b + 1) * RUN)) for b in range(n_steps)]
-        for b in range(n_steps + 2):
-            if b < n_steps:
-                for r in runs[b]:
+        stored = 0
+        for b in range(len(STEPS) + MX_LAG):
+            step = STEPS[b] if b < len(STEPS) else (n_rt + b - len(STEPS),)
+            for r in step:
+                if r < n_rt:
                     transposes(r)
                     if r == 0:
                         transposes(W)
-            for k in range(RUN):
-                if b + 1 < n_steps:
-                    permute(runs[b + 1][k])
-                if b < n_steps:
-                    copy_out(runs[b][k], 0, False)
-                    copy_out(runs[b][k], 1, False)
-                if b == 0 and k == 0:
-                    copy_out(W, 0, True)
-                    copy_out(W, 1, True)
-                    quantise(W)
-                if 0 < b <= n_steps:
-                    quantise(runs[b - 1][k])
-            if b > 1:
-                for r in runs[b - 2]:
-                    multiply(r)
+                    i, k = where[r]
+                    if k == loads[i][3] - 1 and len(x_tiles) < len(loads):
+                        load()
+                if r + PERM_AHEAD < n_rt:
+                    permute(r + PERM_AHEAD)
+                if r < n_rt:
+                    copy_out(r, nc.scalar.copy)
+                    if r == 0:
+                        copy_out(W, nc.vector.tensor_copy)
+                        quantise(W)
+                if 0 <= r - QUANTISE_LAG < n_rt:
+                    quantise(r - QUANTISE_LAG)
+            m = b - MX_LAG
+            if m >= 0:
+                multiply(STEPS[m])
+                outputs(STEPS[m], nc.scalar.copy if m % OUT_SCALAR == OUT_SCALAR - 1 else nc.vector.tensor_copy)
+                while len(x_tiles) == len(loads) and stored < len(stores) and stores[stored][0] // P + stores[stored][1] <= STEPS[m][-1] + 1:
+                    store(*stores[stored])
+                    stored += 1

@@ -18,13 +18,13 @@ K = 2048
 PASSES = 4
 PERM_PASSES = 3
 PW = PERM_PASSES * 256
-GROUPS = [(1,), (1,), (2,), (4,)] + [(4, 4)] * 6 + [(4,), (2,), (1,), (1,)]
+GROUPS = [(1,), (1,), (1, 1), (1, 1, 1, 1)] + [(2, 2, 2, 2)] * 6 + [(2, 2), (2,), (1,), (1,)]
 STEPS = [(0,), (1,)] + [(r, r + 1) for r in range(2, 64, 2)]
-X_BUFS = 6
+X_BUFS = 14
 PERM_AHEAD = 2
 QUANTISE_LAG = 1
 MX_LAG = 2
-OUT_SCALAR = 4
+OUT_SCALAR = 3
 P_BUFS = 5
 G_BUFS = 5
 Q_BUFS = 8

from contextlib import ExitStack

import concourse.mybir as mybir
from concourse.masks import make_identity

FLOPS = 2 * 8192 * 2048 * 128

F32 = mybir.dt.float32
BF16 = mybir.dt.bfloat16
U32 = mybir.dt.uint32
U8 = mybir.dt.uint8
FP8X4 = mybir.dt.float8_e4m3fn_x4
ADD = mybir.AluOpType.add
SUB = mybir.AluOpType.subtract

P = 128
K = 2048
PASSES = 4
PERM_PASSES = 3
PW = PERM_PASSES * 256
GROUPS = [(1,), (1,), (1, 1), (1, 1, 1, 1)] + [(2, 2, 2, 2)] * 6 + [(2, 2), (2,), (1,), (1,)]
STEPS = [(0,), (1,)] + [(r, r + 1) for r in range(2, 64, 2)]
X_BUFS = 14
PERM_AHEAD = 2
QUANTISE_LAG = 1
MX_LAG = 2
OUT_SCALAR = 3
P_BUFS = 5
G_BUFS = 5
Q_BUFS = 8
W = -1


def tile_fftmlp_t_kernel(tc, x, filters_real, filters_imag, out):
    nc = tc.nc
    loads = []
    stores = []
    where = []
    for group in GROUPS:
        base, size = len(where) * P, sum(group)
        stores.append((base, size))
        t0 = 0
        for n in group:
            where += [(len(loads), k) for k in range(n)]
            loads.append((base, size, t0, n))
            t0 += n
    n_rt = len(where)
    assert n_rt * P == x.shape[0]

    with ExitStack() as ctx:
        consts = ctx.enter_context(tc.tile_pool(name="consts", bufs=1))
        xpool = ctx.enter_context(tc.tile_pool(name="xpool", bufs=X_BUFS))
        ppool = ctx.enter_context(tc.tile_pool(name="ppool", bufs=P_BUFS))
        gpool = ctx.enter_context(tc.tile_pool(name="gpool", bufs=G_BUFS))
        qpool = ctx.enter_context(tc.tile_pool(name="qpool", bufs=Q_BUFS))
        psum_t = ctx.enter_context(tc.psum_pool(name="psum_t", bufs=6))
        psum_o = ctx.enter_context(tc.psum_pool(name="psum_o", bufs=2))
        ctx.enter_context(tc.manual_schedule())

        fr = consts.tile([P, K // 2], BF16, name="fr")
        fi = consts.tile([P, K // 2], BF16, name="fi")
        w_sum = consts.tile([P, K], BF16, name="w_sum")
        ident = consts.tile([P, P], F32, name="ident")
        o_all = consts.tile([P, n_rt * P], F32, name="o_all")
        x_tiles = []
        perms = {}
        banks = {}
        grouped = {}
        codes = {}
        scales = {}
        o_banks = {}

        def load():
            base, size, t0, n = loads[len(x_tiles)]
            x_sb = xpool.tile([P, n * K], BF16, tag="x", name="x_sb")
            rows = x[base : base + size * P].rearrange("(p t) c f -> p t (c f)", t=size)
            nc.sync.dma_start(out=x_sb[:].rearrange("p (t k) -> p t k", t=n), in_=rows[:, t0 : t0 + n])
            x_tiles.append(x_sb)

        def rows_of(r):
            if r == W:
                return w_sum[:]
            i, k = where[r]
            return x_tiles[i][:, k * K : (k + 1) * K]

        def permute(r):
            perms[r] = ppool.tile([P, 2 * PW], BF16, tag="perm", name="perm")
            nc.vector.tensor_copy(
                out=perms[r][:].rearrange("p (u b e) -> p u b e", u=2, e=16),
                in_=rows_of(r)[:, : 2 * PW].rearrange("p (b u e) -> p u b e", u=2, e=16),
            )

        def transposes(r):
            plain = rows_of(r).bitcast(F32)
            words = perms[r][:].bitcast(F32)
            for h in range(2):
                bank = psum_t.tile([P, 4, P], F32, tag="xt", name="bank")
                for j in range(4):
                    g, u = 2 * h + j // 2, j % 2
                    if g < PERM_PASSES:
                        w0 = u * (PW // 2) + g * P
                        in_words = words[:, w0 : w0 + P]
                    else:
                        in_words = plain[:, 256 * g + u : 256 * (g + 1) : 2]
                    nc.tensor.transpose(bank[:, j, :], in_words, ident[:])
                banks[(r, h)] = bank

        def copy_out(r, engine_copy):
            grouped[r] = gpool.tile([P, 4 * PASSES * P], BF16, tag="grouped", name="grouped", align_bytes=64)
            dst = grouped[r][:].bitcast(F32).rearrange("p (g r u) -> p g r u", g=PASSES, u=2)
            for h in range(2):
                src = banks[(r, h)][:].rearrange("p (g u) r -> p g r u", u=2)
                engine_copy(out=dst[:, 2 * h : 2 * h + 2], in_=src)

        def quantise(r):
            pool = consts if r == W else qpool
            tag = "w_" if r == W else ""
            codes[r] = pool.tile([P, PASSES * P], U32, tag=tag + "codes", name="codes", align_bytes=64)
            scales[r] = pool.tile([P, PASSES * P], U8, tag=tag + "scales", name="scales", align_bytes=64)
            nc.vector.quantize_mx(out=codes[r][:].bitcast(FP8X4), scales=scales[r][:], in_=grouped[r][:])

        def multiply(step):
            bank = psum_o.tile([P, 4 * P], F32, tag="o", name="o_bank")
            o_banks[step[0]] = bank
            for k, r in enumerate(step):
                for g in range(PASSES):
                    cols = slice(g * P, (g + 1) * P)
                    nc.tensor.matmul_mx(
                        out=bank[:, k * P : (k + 1) * P],
                        lhsT=codes[r][:, cols].bitcast(FP8X4),
                        lhsT_scale=scales[r][:, cols],
                        rhs=codes[W][:, cols].bitcast(FP8X4),
                        rhs_scale=scales[W][:, cols],
                        start=(g == 0),
                        stop=(g == PASSES - 1),
                    )

        def outputs(step, engine_copy):
            r0, n = step[0], len(step)
            engine_copy(out=o_all[:, r0 * P : (r0 + n) * P], in_=o_banks[r0][:, : n * P])

        def store(base, size):
            rows = out[base : base + size * P, :].rearrange("(p t) o -> p (t o)", t=size)
            nc.sync.dma_start(out=rows, in_=o_all[:, base : base + size * P])

        load()
        nc.sync.dma_start(out=fr[:], in_=filters_real)
        nc.sync.dma_start(out=fi[:], in_=filters_imag)
        while len(x_tiles) < X_BUFS:
            load()
        make_identity(nc, ident[:])

        permute(0)
        nc.vector.tensor_tensor(out=w_sum[:, : K // 2], in0=fr[:], in1=fi[:], op=ADD)
        nc.vector.tensor_tensor(out=w_sum[:, K // 2 :], in0=fr[:], in1=fi[:], op=SUB)
        permute(W)
        for r in range(1, PERM_AHEAD):
            permute(r)

        stored = 0
        for b in range(len(STEPS) + MX_LAG):
            step = STEPS[b] if b < len(STEPS) else (n_rt + b - len(STEPS),)
            for r in step:
                if r < n_rt:
                    transposes(r)
                    if r == 0:
                        transposes(W)
                    i, k = where[r]
                    if k == loads[i][3] - 1 and len(x_tiles) < len(loads):
                        load()
                if r + PERM_AHEAD < n_rt:
                    permute(r + PERM_AHEAD)
                if r < n_rt:
                    copy_out(r, nc.scalar.copy)
                    if r == 0:
                        copy_out(W, nc.vector.tensor_copy)
                        quantise(W)
                if 0 <= r - QUANTISE_LAG < n_rt:
                    quantise(r - QUANTISE_LAG)
            m = b - MX_LAG
            if m >= 0:
                multiply(STEPS[m])
                outputs(STEPS[m], nc.scalar.copy if m % OUT_SCALAR == OUT_SCALAR - 1 else nc.vector.tensor_copy)
                while len(x_tiles) == len(loads) and stored < len(stores) and stores[stored][0] // P + stores[stored][1] <= STEPS[m][-1] + 1:
                    store(*stores[stored])
                    stored += 1
